import numpy as np
import ml_dtypes


def mxq(x, axis, fmt="e4m3"):
    dtype, down = {"e4m3": (ml_dtypes.float8_e4m3fn, 7), "e5m2": (ml_dtypes.float8_e5m2, 14)}[fmt]
    v = np.moveaxis(np.asarray(x, np.float32).astype(ml_dtypes.bfloat16).astype(np.float64), axis, -1)
    blocks = v.reshape(v.shape[:-1] + (-1, 32))
    amax = np.abs(blocks).max(-1, keepdims=True)
    byte = np.maximum(np.where(amax > 0, np.frexp(amax)[1] - 1 + 127, 0) - down, 1)
    scale = np.exp2(byte - 127.0)
    codes = (blocks / scale).astype(np.float32).astype(dtype).astype(np.float64)
    return np.moveaxis((codes * scale).reshape(v.shape), -1, axis)


WIDE = False


def mx_kscale(k):
    if not WIDE:
        return np.ones(k)
    levels = np.array([10, -10, 5, -5, 0])
    a = np.random.permutation(np.resize(levels, k // 512 * 4)).reshape(k // 512, 4)
    idx = np.arange(k)
    return np.exp2(a[idx // 512, idx % 128 // 32])


BF16 = ml_dtypes.bfloat16


def bf(x):
    return np.asarray(x, np.float32).astype(BF16)


def f64(x):
    return np.asarray(x).astype(np.float64)


E2M1 = np.array([0.0, 0.5, 1.0, 1.5, 2.0, 3.0, 4.0, 6.0, -0.0, -0.5, -1.0, -1.5, -2.0, -3.0, -4.0, -6.0])


def pack_weight(w, fmt):
    k, n = w.shape
    w = f64(bf(w)).reshape(k // 32, 32, n)
    amax = np.abs(w).max(1)
    if fmt == "e4m3":
        byte = np.frexp(amax)[1] - 1 + 127 - 7
    else:
        mant, ex = np.frexp(amax / 6.0)
        byte = np.where(mant > 0.5, ex, ex - 1) + 127
    byte = np.clip(np.where(amax > 0, byte, 1), 1, 254)
    scaled = (w * np.exp2(127.0 - byte)[:, None, :]).reshape(k, n).astype(np.float32)
    by_word = np.ascontiguousarray(scaled.reshape(k // 512, 128, 4, n).transpose(0, 1, 3, 2))
    if fmt == "e4m3":
        words = by_word.astype(ml_dtypes.float8_e4m3fn).view(np.uint8)
    else:
        c = by_word.astype(ml_dtypes.float4_e2m1fn).view(np.uint8) & 0xF
        words = c[..., 0::2] | (c[..., 1::2] << 4)
    return np.ascontiguousarray(words), np.ascontiguousarray(byte.astype(np.uint8).reshape(k // 512, 16, n))


def unpack_weight(words, scales, fmt):
    g, p, n, _ = words.shape
    if fmt == "e4m3":
        vals = np.ascontiguousarray(words).view(ml_dtypes.float8_e4m3fn).astype(np.float64)
    else:
        nib = np.empty((g, p, n, 4), np.uint8)
        nib[..., 0::2] = words & 0xF
        nib[..., 1::2] = words >> 4
        vals = E2M1[nib]
    vals = vals * np.repeat(np.exp2(scales.astype(np.float64) - 127.0), 8, axis=1)[..., None]
    return vals.transpose(0, 1, 3, 2).reshape(g * 512, n)


B, K, N = 128, 4096, 4096
NACT = 4


def setup_inputs():
    s = mx_kscale(K)
    g = np.tile(np.array([1.0, 1.0, 1.0, 0.5]), N // NACT)
    x = np.random.standard_normal((B, K)) * s
    weight = np.random.uniform(-1.0, 1.0, (N, K)) / np.sqrt(K) * g[:, None] / s[None, :]
    words, scales = pack_weight(weight.T, "e4m3")
    return {"x": bf(x), "weight_words": words, "weight_scales": scales}


def reference(x, weight_words, weight_scales):
    y = mxq(f64(x), 1, "e4m3") @ unpack_weight(weight_words, weight_scales, "e4m3")
    rows, cols = y.shape
    y3 = y.reshape(rows, cols // NACT, NACT)
    out = np.stack(
        [y3[..., 0],
         np.cos(y3[..., 1]),
         np.sin(y3[..., 2]),
         np.tan(y3[..., 3])],
        axis=-1,
    )
    return out.reshape(rows, cols)

@@ -1,0 +1,156 @@
+import math
+from contextlib import ExitStack
+
+import concourse.mybir as mybir
+from concourse.masks import make_identity
+
+F32 = mybir.dt.float32
+BF16 = mybir.dt.bfloat16
+I32 = mybir.dt.int32
+U32 = mybir.dt.uint32
+U8 = mybir.dt.uint8
+FP8X4 = mybir.dt.float8_e4m3fn_x4
+ALU = mybir.AluOpType
+ACT = mybir.ActivationFunctionType
+
+P = 128
+B, K, N = 128, 4096, 4096
+K_PASS = 512
+G = K // K_PASS
+BANK = 512
+FLOPS = 2 * B * K * N
+
+PI = math.pi
+PI_BELOW = 3.1415925025939941
+
+PLAN = [
+    (0, 2048, [(g, 1) for g in range(8)]),
+    (2048, 1024, [(0, 2), (2, 2), (4, 2), (6, 2)]),
+    (3072, 512, [(0, 4), (4, 4)]),
+    (3584, 512, [(0, 4), (4, 3), (7, 1)]),
+]
+MANUAL = False
+N_KT = 3
+
+
+def tile_mylayerfunc_w_kernel(tc, x, weight_words, weight_scales, out):
+    nc = tc.nc
+    with ExitStack() as ctx:
+        if MANUAL:
+            ctx.enter_context(tc.manual_schedule())
+        keep = ctx.enter_context(tc.tile_pool(name="keep", bufs=1))
+        wpool = ctx.enter_context(tc.tile_pool(name="wpool", bufs=1))
+        work = ctx.enter_context(tc.tile_pool(name="work", bufs=3))
+        psum = ctx.enter_context(tc.psum_pool(name="psum", bufs=1))
+
+        planes = keep.tile([P, 2, N], U8, name="planes", align_bytes=64)
+        nc.vector.memset(planes[:].rearrange("p h n -> p (h n)").bitcast(I32), 0)
+        kts = []
+        for i in range(N_KT):
+            kt = keep.tile([P, 4, BANK // 4], I32, name="kt%d" % i)
+            nc.vector.memset(kt[:, 0, :], 0)
+            kts.append(kt)
+        warm = keep.tile([P, 1], F32, name="warm")
+        nc.vector.memset(warm[:], 0.0)
+        warm2 = keep.tile([P, 1], F32, name="warm2")
+        nc.scalar.activation(out=warm2[:], in_=warm[:], func=ACT.Sin)
+        ident = keep.tile([P, P], F32, name="ident")
+        make_identity(nc, ident[:])
+
+        x_sb = keep.tile([P, K], BF16, name="x_sb")
+        nc.sync.dma_start(out=x_sb[:], in_=x)
+        for h in range(2):
+            for q in range(4):
+                nc.sync.dma_start(
+                    out=planes[32 * q : 32 * q + 16, h, :].bitcast(I32),
+                    in_=weight_scales[4 * h : 4 * h + 4, 4 * q : 4 * q + 4, :].bitcast(I32),
+                )
+        w_view = weight_words.rearrange("g p n t -> p g (n t)")
+        w_tiles = {}
+        for r, (c0, width, loads) in enumerate(PLAN):
+            for g0, ng in loads:
+                wt = wpool.tile([P, ng, width], U32, name="w%d_%d" % (r, g0), align_bytes=64)
+                nc.sync.dma_start(
+                    out=wt[:].bitcast(I32),
+                    in_=w_view[:, g0 : g0 + ng, 4 * c0 : 4 * (c0 + width)].bitcast(I32),
+                )
+                for g in range(g0, g0 + ng):
+                    w_tiles[(r, g)] = (wt, g - g0)
+
+        x_words = x_sb[:].bitcast(F32)
+        grouped = keep.tile([P, K], BF16, name="grouped", align_bytes=64)
+        grouped_words = grouped[:].bitcast(F32)
+        x_codes = keep.tile([P, G * B], U32, name="x_codes", align_bytes=64)
+        x_scales = keep.tile([P, G * B], U8, name="x_scales", align_bytes=64)
+        xts = []
+        for j in range(4):
+            xt = psum.tile([P, 4, B], F32, name="xt%d" % j, tag="bank%d" % (4 + j))
+            for i in range(4):
+                g, u = 2 * j + i // 2, i % 2
+                nc.tensor.transpose(xt[:, i, :], x_words[:, 256 * g + u : 256 * (g + 1) : 2], ident[:])
+            xts.append(xt)
+        for j in range(4):
+            dst = grouped_words[:, 512 * j : 512 * (j + 1)].rearrange("p (g b u) -> p g b u", g=2, u=2)
+            src = xts[j][:].rearrange("p (g u) b -> p g b u", u=2)
+            if j % 2 == 0:
+                nc.vector.tensor_copy(out=dst, in_=src)
+            else:
+                nc.scalar.copy(out=dst, in_=src)
+        for h in range(2):
+            nc.vector.quantize_mx(
+                out=x_codes[:, 512 * h : 512 * (h + 1)].bitcast(FP8X4),
+                scales=x_scales[:, 512 * h : 512 * (h + 1)],
+                in_=grouped[:, 2048 * h : 2048 * (h + 1)],
+            )
+
+        o_all = keep.tile([P, N], F32, name="o_all")
+        count = [0]
+
+        def finish(acc, c0, n):
+            ln = n // 4
+            yv = acc[:, 0:n].rearrange("p (n c) -> p c n", c=4)
+            kt = kts[count[0] % N_KT]
+            count[0] += 1
+            t = work.tile([P, 4, ln], F32, name="t", tag="t")
+            cs3 = work.tile([P, ln], F32, name="cs3", tag="cs3")
+            rc3 = work.tile([P, ln], F32, name="rc3", tag="rc3")
+            nc.vector.tensor_scalar(out=kt[:, 3, 0:ln], in0=yv[:, 3, :], scalar1=1.0 / PI, scalar2=0.25, op0=ALU.mult, op1=ALU.add)
+            nc.vector.scalar_tensor_tensor(out=t[:, 3, :], in0=kt[:, 3, 0:ln], scalar=-PI, in1=yv[:, 3, :], op0=ALU.mult, op1=ALU.add)
+            nc.scalar.activation(out=cs3[:], in_=t[:, 3, :], func=ACT.Sin, bias=PI / 2)
+            nc.scalar.activation(out=t[:, 3, :], in_=t[:, 3, :], func=ACT.Sin)
+            nc.vector.tensor_scalar(out=kt[:, 1:3, 0:ln], in0=yv[:, 1:3, :], scalar1=0.5 / PI, scalar2=0.0, op0=ALU.mult, op1=ALU.add)
+            nc.vector.scalar_tensor_tensor(out=t[:, 0:3, :], in0=kt[:, 0:3, 0:ln], scalar=-2.0 * PI, in1=yv[:, 0:3, :], op0=ALU.mult, op1=ALU.add)
+            nc.scalar.activation(out=t[:, 1, :], in_=t[:, 1, :], func=ACT.Abs)
+            nc.scalar.activation(out=t[:, 1, :], in_=t[:, 1, :], func=ACT.Sin, bias=PI / 2, scale=-1.0)
+            nc.gpsimd.tensor_scalar(out=t[:, 2, :], in0=t[:, 2, :], scalar1=PI_BELOW, scalar2=-PI_BELOW, op0=ALU.min, op1=ALU.max)
+            nc.scalar.activation(out=t[:, 2, :], in_=t[:, 2, :], func=ACT.Sin)
+            nc.vector.reciprocal(out=rc3[:], in_=cs3[:])
+            nc.vector.tensor_tensor(out=t[:, 3, :], in0=t[:, 3, :], in1=rc3[:], op=ALU.mult)
+            nc.vector.tensor_copy(
+                out=o_all[:, c0 : c0 + n].rearrange("p (n c) -> p n c", c=4),
+                in_=t[:].rearrange("p c n -> p n c"),
+            )
+            nc.sync.dma_start(out=out[:, c0 : c0 + n], in_=o_all[:, c0 : c0 + n])
+
+        for r, (c0, width, loads) in enumerate(PLAN):
+            banks = width // BANK
+            accs = []
+            for i in range(banks):
+                bank = (c0 + i * BANK) // BANK
+                acc = psum.tile([P, BANK], F32, name="acc%d" % bank, tag="bank%d" % bank)
+                accs.append(acc)
+            for g in range(G):
+                wt, gi = w_tiles[(r, g)]
+                h, j = g // 4, g % 4
+                for i in range(banks):
+                    nc.tensor.matmul_mx(
+                        out=accs[i][:],
+                        lhsT=x_codes[:, B * g : B * (g + 1)].bitcast(FP8X4),
+                        lhsT_scale=x_scales[:, B * g : B * (g + 1)],
+                        rhs=wt[:, gi, BANK * i : BANK * (i + 1)].bitcast(FP8X4),
+                        rhs_scale=planes[4 * j : P, h, c0 + BANK * i : c0 + BANK * (i + 1)],
+                        start=(g == 0),
+                        stop=(g == G - 1),
+                    )
+            for i in range(banks):
+                finish(accs[i], c0 + BANK * i, BANK)

@@ -59,8 +59,8 @@ def tile_mylayerfunc_w_kernel(tc, x, weight_words, weight_scales, out):
 
         x_sb = keep.tile([P, K], BF16, name="x_sb")
         nc.sync.dma_start(out=x_sb[:], in_=x)
-        for h in range(2):
-            for q in range(4):
+        for q in (2, 3, 0, 1):
+            for h in range(2):
                 nc.sync.dma_start(
                     out=planes[32 * q : 32 * q + 16, h, :].bitcast(I32),
                     in_=weight_scales[4 * h : 4 * h + 4, 4 * q : 4 * q + 4, :].bitcast(I32),

@@ -24,10 +24,10 @@ PI = math.pi
 PI_BELOW = 3.1415925025939941
 
 PLAN = [
-    (0, 2048, [(g, 1) for g in range(8)]),
-    (2048, 1024, [(0, 2), (2, 2), (4, 2), (6, 2)]),
+    (0, 2048, [(0, 4), (4, 2), (6, 1), (7, 1)]),
+    (2048, 1024, [(0, 4), (4, 2), (6, 2)]),
     (3072, 512, [(0, 4), (4, 4)]),
-    (3584, 512, [(0, 4), (4, 3), (7, 1)]),
+    (3584, 512, [(0, 5), (5, 2), (7, 1)]),
 ]
 MANUAL = False
 N_KT = 3
@@ -48,7 +48,6 @@ def tile_mylayerfunc_w_kernel(tc, x, weight_words, weight_scales, out):
         kts = []
         for i in range(N_KT):
             kt = keep.tile([P, 4, BANK // 4], I32, name="kt%d" % i)
-            nc.vector.memset(kt[:, 0, :], 0)
             kts.append(kt)
         warm = keep.tile([P, 1], F32, name="warm")
         nc.vector.memset(warm[:], 0.0)
@@ -106,7 +105,7 @@ def tile_mylayerfunc_w_kernel(tc, x, weight_words, weight_scales, out):
         o_all = keep.tile([P, N], F32, name="o_all")
         count = [0]
 
-        def finish(acc, c0, n):
+        def finish(acc, c0, n, last):
             ln = n // 4
             yv = acc[:, 0:n].rearrange("p (n c) -> p c n", c=4)
             kt = kts[count[0] % N_KT]
@@ -119,14 +118,16 @@ def tile_mylayerfunc_w_kernel(tc, x, weight_words, weight_scales, out):
             nc.scalar.activation(out=cs3[:], in_=t[:, 3, :], func=ACT.Sin, bias=PI / 2)
             nc.scalar.activation(out=t[:, 3, :], in_=t[:, 3, :], func=ACT.Sin)
             nc.vector.tensor_scalar(out=kt[:, 1:3, 0:ln], in0=yv[:, 1:3, :], scalar1=0.5 / PI, scalar2=0.0, op0=ALU.mult, op1=ALU.add)
-            nc.vector.scalar_tensor_tensor(out=t[:, 0:3, :], in0=kt[:, 0:3, 0:ln], scalar=-2.0 * PI, in1=yv[:, 0:3, :], op0=ALU.mult, op1=ALU.add)
+            nc.vector.scalar_tensor_tensor(out=t[:, 1:3, :], in0=kt[:, 1:3, 0:ln], scalar=-2.0 * PI, in1=yv[:, 1:3, :], op0=ALU.mult, op1=ALU.add)
+            nc.scalar.copy(out=t[:, 0, :], in_=yv[:, 0, :])
             nc.scalar.activation(out=t[:, 1, :], in_=t[:, 1, :], func=ACT.Abs)
             nc.scalar.activation(out=t[:, 1, :], in_=t[:, 1, :], func=ACT.Sin, bias=PI / 2, scale=-1.0)
             nc.gpsimd.tensor_scalar(out=t[:, 2, :], in0=t[:, 2, :], scalar1=PI_BELOW, scalar2=-PI_BELOW, op0=ALU.min, op1=ALU.max)
             nc.scalar.activation(out=t[:, 2, :], in_=t[:, 2, :], func=ACT.Sin)
             nc.vector.reciprocal(out=rc3[:], in_=cs3[:])
             nc.vector.tensor_tensor(out=t[:, 3, :], in0=t[:, 3, :], in1=rc3[:], op=ALU.mult)
-            nc.vector.tensor_copy(
+            interleave = nc.vector.tensor_copy if last else nc.scalar.copy
+            interleave(
                 out=o_all[:, c0 : c0 + n].rearrange("p (n c) -> p n c", c=4),
                 in_=t[:].rearrange("p c n -> p n c"),
             )
@@ -153,4 +154,4 @@ def tile_mylayerfunc_w_kernel(tc, x, weight_words, weight_scales, out):
                         stop=(g == G - 1),
                     )
             for i in range(banks):
-                finish(accs[i], c0 + BANK * i, BANK)
+                finish(accs[i], c0 + BANK * i, BANK, r == len(PLAN) - 1)

@@ -26,7 +26,7 @@ PI_BELOW = 3.1415925025939941
 PLAN = [
     (0, 2048, [(0, 4), (4, 2), (6, 1), (7, 1)]),
     (2048, 1024, [(0, 4), (4, 2), (6, 2)]),
-    (3072, 512, [(0, 4), (4, 4)]),
+    (3072, 512, [(0, 6), (6, 2)]),
     (3584, 512, [(0, 5), (5, 2), (7, 1)]),
 ]
 MANUAL = False
@@ -114,10 +114,10 @@ def tile_mylayerfunc_w_kernel(tc, x, weight_words, weight_scales, out):
             cs3 = work.tile([P, ln], F32, name="cs3", tag="cs3")
             rc3 = work.tile([P, ln], F32, name="rc3", tag="rc3")
             nc.vector.tensor_scalar(out=kt[:, 3, 0:ln], in0=yv[:, 3, :], scalar1=1.0 / PI, scalar2=0.25, op0=ALU.mult, op1=ALU.add)
+            nc.vector.tensor_scalar(out=kt[:, 1:3, 0:ln], in0=yv[:, 1:3, :], scalar1=0.5 / PI, scalar2=0.0, op0=ALU.mult, op1=ALU.add)
             nc.vector.scalar_tensor_tensor(out=t[:, 3, :], in0=kt[:, 3, 0:ln], scalar=-PI, in1=yv[:, 3, :], op0=ALU.mult, op1=ALU.add)
             nc.scalar.activation(out=cs3[:], in_=t[:, 3, :], func=ACT.Sin, bias=PI / 2)
             nc.scalar.activation(out=t[:, 3, :], in_=t[:, 3, :], func=ACT.Sin)
-            nc.vector.tensor_scalar(out=kt[:, 1:3, 0:ln], in0=yv[:, 1:3, :], scalar1=0.5 / PI, scalar2=0.0, op0=ALU.mult, op1=ALU.add)
             nc.vector.scalar_tensor_tensor(out=t[:, 1:3, :], in0=kt[:, 1:3, 0:ln], scalar=-2.0 * PI, in1=yv[:, 1:3, :], op0=ALU.mult, op1=ALU.add)
             nc.scalar.copy(out=t[:, 0, :], in_=yv[:, 0, :])
             nc.scalar.activation(out=t[:, 1, :], in_=t[:, 1, :], func=ACT.Abs)

@@ -105,7 +105,7 @@ def tile_mylayerfunc_w_kernel(tc, x, weight_words, weight_scales, out):
         o_all = keep.tile([P, N], F32, name="o_all")
         count = [0]
 
-        def finish(acc, c0, n, last):
+        def finish(acc, c0, n, alone, last):
             ln = n // 4
             yv = acc[:, 0:n].rearrange("p (n c) -> p c n", c=4)
             kt = kts[count[0] % N_KT]
@@ -124,14 +124,20 @@ def tile_mylayerfunc_w_kernel(tc, x, weight_words, weight_scales, out):
             nc.scalar.activation(out=t[:, 1, :], in_=t[:, 1, :], func=ACT.Sin, bias=PI / 2, scale=-1.0)
             nc.gpsimd.tensor_scalar(out=t[:, 2, :], in0=t[:, 2, :], scalar1=PI_BELOW, scalar2=-PI_BELOW, op0=ALU.min, op1=ALU.max)
             nc.scalar.activation(out=t[:, 2, :], in_=t[:, 2, :], func=ACT.Sin)
-            nc.vector.reciprocal(out=rc3[:], in_=cs3[:])
-            nc.vector.tensor_tensor(out=t[:, 3, :], in0=t[:, 3, :], in1=rc3[:], op=ALU.mult)
+            parts = 2 if alone else 1
+            step = ln // parts
+            cuts = [(step * i, step * (i + 1)) for i in range(parts)]
+            for a, b in cuts:
+                nc.vector.reciprocal(out=rc3[:, a:b], in_=cs3[:, a:b])
+            for a, b in cuts:
+                nc.vector.tensor_tensor(out=t[:, 3, a:b], in0=t[:, 3, a:b], in1=rc3[:, a:b], op=ALU.mult)
             interleave = nc.vector.tensor_copy if last else nc.scalar.copy
-            interleave(
-                out=o_all[:, c0 : c0 + n].rearrange("p (n c) -> p n c", c=4),
-                in_=t[:].rearrange("p c n -> p n c"),
-            )
-            nc.sync.dma_start(out=out[:, c0 : c0 + n], in_=o_all[:, c0 : c0 + n])
+            for a, b in cuts:
+                interleave(
+                    out=o_all[:, c0 + 4 * a : c0 + 4 * b].rearrange("p (n c) -> p n c", c=4),
+                    in_=t[:, :, a:b].rearrange("p c n -> p n c"),
+                )
+                nc.sync.dma_start(out=out[:, c0 + 4 * a : c0 + 4 * b], in_=o_all[:, c0 + 4 * a : c0 + 4 * b])
 
         for r, (c0, width, loads) in enumerate(PLAN):
             banks = width // BANK
@@ -154,4 +160,4 @@ def tile_mylayerfunc_w_kernel(tc, x, weight_words, weight_scales, out):
                         stop=(g == G - 1),
                     )
             for i in range(banks):
-                finish(accs[i], c0 + BANK * i, BANK, r == len(PLAN) - 1)
+                finish(accs[i], c0 + BANK * i, BANK, banks == 1, r == len(PLAN) - 1)

@@ -24,10 +24,10 @@ PI = math.pi
 PI_BELOW = 3.1415925025939941
 
 PLAN = [
-    (0, 2048, [(0, 4), (4, 2), (6, 1), (7, 1)]),
-    (2048, 1024, [(0, 4), (4, 2), (6, 2)]),
-    (3072, 512, [(0, 6), (6, 2)]),
-    (3584, 512, [(0, 5), (5, 2), (7, 1)]),
+    (0, [512, 512, 512, 512, 128], [(0, 4), (4, 2), (6, 1), (7, 1)]),
+    (2176, [512, 512], [(0, 4), (4, 2), (6, 2)]),
+    (3200, [512], [(0, 6), (6, 2)]),
+    (3712, [256, 128], [(0, 5), (5, 2), (7, 1)]),
 ]
 MANUAL = False
 N_KT = 3
@@ -66,7 +66,8 @@ def tile_mylayerfunc_w_kernel(tc, x, weight_words, weight_scales, out):
                 )
         w_view = weight_words.rearrange("g p n t -> p g (n t)")
         w_tiles = {}
-        for r, (c0, width, loads) in enumerate(PLAN):
+        for r, (c0, widths, loads) in enumerate(PLAN):
+            width = sum(widths)
             for g0, ng in loads:
                 wt = wpool.tile([P, ng, width], U32, name="w%d_%d" % (r, g0), align_bytes=64)
                 nc.sync.dma_start(
@@ -139,25 +140,27 @@ def tile_mylayerfunc_w_kernel(tc, x, weight_words, weight_scales, out):
                 )
                 nc.sync.dma_start(out=out[:, c0 + 4 * a : c0 + 4 * b], in_=o_all[:, c0 + 4 * a : c0 + 4 * b])
 
-        for r, (c0, width, loads) in enumerate(PLAN):
-            banks = width // BANK
+        next_bank = 0
+        for r, (c0, widths, loads) in enumerate(PLAN):
             accs = []
-            for i in range(banks):
-                bank = (c0 + i * BANK) // BANK
-                acc = psum.tile([P, BANK], F32, name="acc%d" % bank, tag="bank%d" % bank)
+            starts = []
+            for i, n_mm in enumerate(widths):
+                acc = psum.tile([P, BANK], F32, name="acc%d_%d" % (r, i), tag="bank%d" % (next_bank % 8))
+                next_bank += 1
                 accs.append(acc)
+                starts.append(sum(widths[0:i]))
             for g in range(G):
                 wt, gi = w_tiles[(r, g)]
                 h, j = g // 4, g % 4
-                for i in range(banks):
+                for i, n_mm in enumerate(widths):
                     nc.tensor.matmul_mx(
-                        out=accs[i][:],
+                        out=accs[i][:, 0:n_mm],
                         lhsT=x_codes[:, B * g : B * (g + 1)].bitcast(FP8X4),
                         lhsT_scale=x_scales[:, B * g : B * (g + 1)],
-                        rhs=wt[:, gi, BANK * i : BANK * (i + 1)].bitcast(FP8X4),
-                        rhs_scale=planes[4 * j : P, h, c0 + BANK * i : c0 + BANK * (i + 1)],
+                        rhs=wt[:, gi, starts[i] : starts[i] + n_mm].bitcast(FP8X4),
+                        rhs_scale=planes[4 * j : P, h, c0 + starts[i] : c0 + starts[i] + n_mm],
                         start=(g == 0),
                         stop=(g == G - 1),
                     )
-            for i in range(banks):
-                finish(accs[i], c0 + BANK * i, BANK, banks == 1, r == len(PLAN) - 1)
+            for i, n_mm in enumerate(widths):
+                finish(accs[i], c0 + starts[i], n_mm, len(widths) == 1, r == len(PLAN) - 1)

@@ -29,15 +29,14 @@ PLAN = [
     (3200, [512], [(0, 6), (6, 2)]),
     (3712, [256, 128], [(0, 5), (5, 2), (7, 1)]),
 ]
-MANUAL = False
+FILLERS = [8, 6, 0, 0]
 N_KT = 3
 
 
 def tile_mylayerfunc_w_kernel(tc, x, weight_words, weight_scales, out):
     nc = tc.nc
     with ExitStack() as ctx:
-        if MANUAL:
-            ctx.enter_context(tc.manual_schedule())
+        ctx.enter_context(tc.manual_schedule(engines={mybir.EngineType.PE}))
         keep = ctx.enter_context(tc.tile_pool(name="keep", bufs=1))
         wpool = ctx.enter_context(tc.tile_pool(name="wpool", bufs=1))
         work = ctx.enter_context(tc.tile_pool(name="work", bufs=3))
@@ -162,5 +161,9 @@ def tile_mylayerfunc_w_kernel(tc, x, weight_words, weight_scales, out):
                         start=(g == 0),
                         stop=(g == G - 1),
                     )
+            if FILLERS[r] > 0:
+                idle = psum.tile([P, BANK], F32, name="idle%d" % r, tag="bank7")
+                for i in range(FILLERS[r]):
+                    nc.tensor.matmul(out=idle[:], lhsT=x_sb[:, 0:P], rhs=x_sb[:, 0:BANK], start=True, stop=True)
             for i, n_mm in enumerate(widths):
                 finish(accs[i], c0 + starts[i], n_mm, len(widths) == 1, r == len(PLAN) - 1)

@@ -105,20 +105,30 @@ def tile_mylayerfunc_w_kernel(tc, x, weight_words, weight_scales, out):
         o_all = keep.tile([P, N], F32, name="o_all")
         count = [0]
 
-        def finish(acc, c0, n, alone, last):
-            ln = n // 4
-            yv = acc[:, 0:n].rearrange("p (n c) -> p c n", c=4)
-            kt = kts[count[0] % N_KT]
-            count[0] += 1
-            t = work.tile([P, 4, ln], F32, name="t", tag="t")
-            cs3 = work.tile([P, ln], F32, name="cs3", tag="cs3")
-            rc3 = work.tile([P, ln], F32, name="rc3", tag="rc3")
-            nc.vector.tensor_scalar(out=kt[:, 3, 0:ln], in0=yv[:, 3, :], scalar1=1.0 / PI, scalar2=0.25, op0=ALU.mult, op1=ALU.add)
-            nc.vector.tensor_scalar(out=kt[:, 1:3, 0:ln], in0=yv[:, 1:3, :], scalar1=0.5 / PI, scalar2=0.0, op0=ALU.mult, op1=ALU.add)
-            nc.vector.scalar_tensor_tensor(out=t[:, 3, :], in0=kt[:, 3, 0:ln], scalar=-PI, in1=yv[:, 3, :], op0=ALU.mult, op1=ALU.add)
+        def finish_all(groups, last):
+            work_of = []
+            for acc, c0, n in groups:
+                ln = n // 4
+                kt = kts[count[0] % N_KT]
+                count[0] += 1
+                t = work.tile([P, 4, ln], F32, name="t", tag="t")
+                cs3 = work.tile([P, ln], F32, name="cs3", tag="cs3")
+                rc3 = work.tile([P, ln], F32, name="rc3", tag="rc3")
+                work_of.append((acc[:, 0:n].rearrange("p (n c) -> p c n", c=4), kt, t, cs3, rc3, c0, ln))
+            for yv, kt, t, cs3, rc3, c0, ln in work_of:
+                nc.vector.tensor_scalar(out=kt[:, 3, 0:ln], in0=yv[:, 3, :], scalar1=1.0 / PI, scalar2=0.25, op0=ALU.mult, op1=ALU.add)
+            for yv, kt, t, cs3, rc3, c0, ln in work_of:
+                nc.vector.tensor_scalar(out=kt[:, 1:3, 0:ln], in0=yv[:, 1:3, :], scalar1=0.5 / PI, scalar2=0.0, op0=ALU.mult, op1=ALU.add)
+            for yv, kt, t, cs3, rc3, c0, ln in work_of:
+                nc.vector.scalar_tensor_tensor(out=t[:, 3, :], in0=kt[:, 3, 0:ln], scalar=-PI, in1=yv[:, 3, :], op0=ALU.mult, op1=ALU.add)
+            for yv, kt, t, cs3, rc3, c0, ln in work_of:
+                nc.vector.scalar_tensor_tensor(out=t[:, 1:3, :], in0=kt[:, 1:3, 0:ln], scalar=-2.0 * PI, in1=yv[:, 1:3, :], op0=ALU.mult, op1=ALU.add)
+            for yv, kt, t, cs3, rc3, c0, ln in work_of:
+                finish(yv, t, cs3, rc3, c0, ln, len(groups) == 1 and len(widths) == 1, last)
+
+        def finish(yv, t, cs3, rc3, c0, ln, alone, last):
             nc.scalar.activation(out=cs3[:], in_=t[:, 3, :], func=ACT.Sin, bias=PI / 2)
             nc.scalar.activation(out=t[:, 3, :], in_=t[:, 3, :], func=ACT.Sin)
-            nc.vector.scalar_tensor_tensor(out=t[:, 1:3, :], in0=kt[:, 1:3, 0:ln], scalar=-2.0 * PI, in1=yv[:, 1:3, :], op0=ALU.mult, op1=ALU.add)
             nc.scalar.copy(out=t[:, 0, :], in_=yv[:, 0, :])
             nc.scalar.activation(out=t[:, 1, :], in_=t[:, 1, :], func=ACT.Abs)
             nc.scalar.activation(out=t[:, 1, :], in_=t[:, 1, :], func=ACT.Sin, bias=PI / 2, scale=-1.0)
@@ -165,5 +175,9 @@ def tile_mylayerfunc_w_kernel(tc, x, weight_words, weight_scales, out):
                 idle = psum.tile([P, BANK], F32, name="idle%d" % r, tag="bank7")
                 for i in range(FILLERS[r]):
                     nc.tensor.matmul(out=idle[:], lhsT=x_sb[:, 0:P], rhs=x_sb[:, 0:BANK], start=True, stop=True)
-            for i, n_mm in enumerate(widths):
-                finish(accs[i], c0 + starts[i], n_mm, len(widths) == 1, r == len(PLAN) - 1)
+            groups = [(accs[i], c0 + starts[i], n_mm) for i, n_mm in enumerate(widths)]
+            if r == len(PLAN) - 1:
+                finish_all(groups, True)
+            else:
+                for group in groups:
+                    finish_all([group], False)

import math
from contextlib import ExitStack

import concourse.mybir as mybir
from concourse.masks import make_identity

F32 = mybir.dt.float32
BF16 = mybir.dt.bfloat16
I32 = mybir.dt.int32
U32 = mybir.dt.uint32
U8 = mybir.dt.uint8
FP8X4 = mybir.dt.float8_e4m3fn_x4
ALU = mybir.AluOpType
ACT = mybir.ActivationFunctionType

P = 128
B, K, N = 128, 4096, 4096
K_PASS = 512
G = K // K_PASS
BANK = 512
FLOPS = 2 * B * K * N

PI = math.pi
PI_BELOW = 3.1415925025939941

PLAN = [
    (0, [512, 512, 512, 512, 128], [(0, 4), (4, 2), (6, 1), (7, 1)]),
    (2176, [512, 512], [(0, 4), (4, 2), (6, 2)]),
    (3200, [512], [(0, 6), (6, 2)]),
    (3712, [256, 128], [(0, 5), (5, 2), (7, 1)]),
]
FILLERS = [8, 6, 0, 0]
N_KT = 3


def tile_mylayerfunc_w_kernel(tc, x, weight_words, weight_scales, out):
    nc = tc.nc
    with ExitStack() as ctx:
        ctx.enter_context(tc.manual_schedule(engines={mybir.EngineType.PE}))
        keep = ctx.enter_context(tc.tile_pool(name="keep", bufs=1))
        wpool = ctx.enter_context(tc.tile_pool(name="wpool", bufs=1))
        work = ctx.enter_context(tc.tile_pool(name="work", bufs=3))
        psum = ctx.enter_context(tc.psum_pool(name="psum", bufs=1))

        planes = keep.tile([P, 2, N], U8, name="planes", align_bytes=64)
        nc.vector.memset(planes[:].rearrange("p h n -> p (h n)").bitcast(I32), 0)
        kts = []
        for i in range(N_KT):
            kt = keep.tile([P, 4, BANK // 4], I32, name="kt%d" % i)
            kts.append(kt)
        warm = keep.tile([P, 1], F32, name="warm")
        nc.vector.memset(warm[:], 0.0)
        warm2 = keep.tile([P, 1], F32, name="warm2")
        nc.scalar.activation(out=warm2[:], in_=warm[:], func=ACT.Sin)
        ident = keep.tile([P, P], F32, name="ident")
        make_identity(nc, ident[:])

        x_sb = keep.tile([P, K], BF16, name="x_sb")
        nc.sync.dma_start(out=x_sb[:], in_=x)
        for q in (2, 3, 0, 1):
            for h in range(2):
                nc.sync.dma_start(
                    out=planes[32 * q : 32 * q + 16, h, :].bitcast(I32),
                    in_=weight_scales[4 * h : 4 * h + 4, 4 * q : 4 * q + 4, :].bitcast(I32),
                )
        w_view = weight_words.rearrange("g p n t -> p g (n t)")
        w_tiles = {}
        for r, (c0, widths, loads) in enumerate(PLAN):
            width = sum(widths)
            for g0, ng in loads:
                wt = wpool.tile([P, ng, width], U32, name="w%d_%d" % (r, g0), align_bytes=64)
                nc.sync.dma_start(
                    out=wt[:].bitcast(I32),
                    in_=w_view[:, g0 : g0 + ng, 4 * c0 : 4 * (c0 + width)].bitcast(I32),
                )
                for g in range(g0, g0 + ng):
                    w_tiles[(r, g)] = (wt, g - g0)

        x_words = x_sb[:].bitcast(F32)
        grouped = keep.tile([P, K], BF16, name="grouped", align_bytes=64)
        grouped_words = grouped[:].bitcast(F32)
        x_codes = keep.tile([P, G * B], U32, name="x_codes", align_bytes=64)
        x_scales = keep.tile([P, G * B], U8, name="x_scales", align_bytes=64)
        xts = []
        for j in range(4):
            xt = psum.tile([P, 4, B], F32, name="xt%d" % j, tag="bank%d" % (4 + j))
            for i in range(4):
                g, u = 2 * j + i // 2, i % 2
                nc.tensor.transpose(xt[:, i, :], x_words[:, 256 * g + u : 256 * (g + 1) : 2], ident[:])
            xts.append(xt)
        for j in range(4):
            dst = grouped_words[:, 512 * j : 512 * (j + 1)].rearrange("p (g b u) -> p g b u", g=2, u=2)
            src = xts[j][:].rearrange("p (g u) b -> p g b u", u=2)
            if j % 2 == 0:
                nc.vector.tensor_copy(out=dst, in_=src)
            else:
                nc.scalar.copy(out=dst, in_=src)
        for h in range(2):
            nc.vector.quantize_mx(
                out=x_codes[:, 512 * h : 512 * (h + 1)].bitcast(FP8X4),
                scales=x_scales[:, 512 * h : 512 * (h + 1)],
                in_=grouped[:, 2048 * h : 2048 * (h + 1)],
            )

        o_all = keep.tile([P, N], F32, name="o_all")
        count = [0]

        def finish_all(groups, last):
            work_of = []
            for acc, c0, n in groups:
                ln = n // 4
                kt = kts[count[0] % N_KT]
                count[0] += 1
                t = work.tile([P, 4, ln], F32, name="t", tag="t")
                cs3 = work.tile([P, ln], F32, name="cs3", tag="cs3")
                rc3 = work.tile([P, ln], F32, name="rc3", tag="rc3")
                work_of.append((acc[:, 0:n].rearrange("p (n c) -> p c n", c=4), kt, t, cs3, rc3, c0, ln))
            for yv, kt, t, cs3, rc3, c0, ln in work_of:
                nc.vector.tensor_scalar(out=kt[:, 3, 0:ln], in0=yv[:, 3, :], scalar1=1.0 / PI, scalar2=0.25, op0=ALU.mult, op1=ALU.add)
            for yv, kt, t, cs3, rc3, c0, ln in work_of:
                nc.vector.tensor_scalar(out=kt[:, 1:3, 0:ln], in0=yv[:, 1:3, :], scalar1=0.5 / PI, scalar2=0.0, op0=ALU.mult, op1=ALU.add)
            for yv, kt, t, cs3, rc3, c0, ln in work_of:
                nc.vector.scalar_tensor_tensor(out=t[:, 3, :], in0=kt[:, 3, 0:ln], scalar=-PI, in1=yv[:, 3, :], op0=ALU.mult, op1=ALU.add)
            for yv, kt, t, cs3, rc3, c0, ln in work_of:
                nc.vector.scalar_tensor_tensor(out=t[:, 1:3, :], in0=kt[:, 1:3, 0:ln], scalar=-2.0 * PI, in1=yv[:, 1:3, :], op0=ALU.mult, op1=ALU.add)
            for yv, kt, t, cs3, rc3, c0, ln in work_of:
                finish(yv, t, cs3, rc3, c0, ln, len(groups) == 1 and len(widths) == 1, last)

        def finish(yv, t, cs3, rc3, c0, ln, alone, last):
            nc.scalar.activation(out=cs3[:], in_=t[:, 3, :], func=ACT.Sin, bias=PI / 2)
            nc.scalar.activation(out=t[:, 3, :], in_=t[:, 3, :], func=ACT.Sin)
            nc.scalar.copy(out=t[:, 0, :], in_=yv[:, 0, :])
            nc.scalar.activation(out=t[:, 1, :], in_=t[:, 1, :], func=ACT.Abs)
            nc.scalar.activation(out=t[:, 1, :], in_=t[:, 1, :], func=ACT.Sin, bias=PI / 2, scale=-1.0)
            nc.gpsimd.tensor_scalar(out=t[:, 2, :], in0=t[:, 2, :], scalar1=PI_BELOW, scalar2=-PI_BELOW, op0=ALU.min, op1=ALU.max)
            nc.scalar.activation(out=t[:, 2, :], in_=t[:, 2, :], func=ACT.Sin)
            parts = 2 if alone else 1
            step = ln // parts
            cuts = [(step * i, step * (i + 1)) for i in range(parts)]
            for a, b in cuts:
                nc.vector.reciprocal(out=rc3[:, a:b], in_=cs3[:, a:b])
            for a, b in cuts:
                nc.vector.tensor_tensor(out=t[:, 3, a:b], in0=t[:, 3, a:b], in1=rc3[:, a:b], op=ALU.mult)
            interleave = nc.vector.tensor_copy if last else nc.scalar.copy
            for a, b in cuts:
                interleave(
                    out=o_all[:, c0 + 4 * a : c0 + 4 * b].rearrange("p (n c) -> p n c", c=4),
                    in_=t[:, :, a:b].rearrange("p c n -> p n c"),
                )
                nc.sync.dma_start(out=out[:, c0 + 4 * a : c0 + 4 * b], in_=o_all[:, c0 + 4 * a : c0 + 4 * b])

        next_bank = 0
        for r, (c0, widths, loads) in enumerate(PLAN):
            accs = []
            starts = []
            for i, n_mm in enumerate(widths):
                acc = psum.tile([P, BANK], F32, name="acc%d_%d" % (r, i), tag="bank%d" % (next_bank % 8))
                next_bank += 1
                accs.append(acc)
                starts.append(sum(widths[0:i]))
            for g in range(G):
                wt, gi = w_tiles[(r, g)]
                h, j = g // 4, g % 4
                for i, n_mm in enumerate(widths):
                    nc.tensor.matmul_mx(
                        out=accs[i][:, 0:n_mm],
                        lhsT=x_codes[:, B * g : B * (g + 1)].bitcast(FP8X4),
                        lhsT_scale=x_scales[:, B * g : B * (g + 1)],
                        rhs=wt[:, gi, starts[i] : starts[i] + n_mm].bitcast(FP8X4),
                        rhs_scale=planes[4 * j : P, h, c0 + starts[i] : c0 + starts[i] + n_mm],
                        start=(g == 0),
                        stop=(g == G - 1),
                    )
            if FILLERS[r] > 0:
                idle = psum.tile([P, BANK], F32, name="idle%d" % r, tag="bank7")
                for i in range(FILLERS[r]):
                    nc.tensor.matmul(out=idle[:], lhsT=x_sb[:, 0:P], rhs=x_sb[:, 0:BANK], start=True, stop=True)
            groups = [(accs[i], c0 + starts[i], n_mm) for i, n_mm in enumerate(widths)]
            if r == len(PLAN) - 1:
                finish_all(groups, True)
            else:
                for group in groups:
                    finish_all([group], False)
